import numpy as np
import ml_dtypes


def mxq(x, axis, fmt="e4m3"):
    dtype, down = {"e4m3": (ml_dtypes.float8_e4m3fn, 7), "e5m2": (ml_dtypes.float8_e5m2, 14)}[fmt]
    v = np.moveaxis(np.asarray(x, np.float32).astype(ml_dtypes.bfloat16).astype(np.float64), axis, -1)
    blocks = v.reshape(v.shape[:-1] + (-1, 32))
    amax = np.abs(blocks).max(-1, keepdims=True)
    byte = np.maximum(np.where(amax > 0, np.frexp(amax)[1] - 1 + 127, 0) - down, 1)
    scale = np.exp2(byte - 127.0)
    codes = (blocks / scale).astype(np.float32).astype(dtype).astype(np.float64)
    return np.moveaxis((codes * scale).reshape(v.shape), -1, axis)


WIDE = False


def mx_kscale(k):
    if not WIDE:
        return np.ones(k)
    levels = np.array([10, -10, 5, -5, 0])
    if k % 512:
        return np.exp2(np.random.permutation(np.resize(levels, k // 32))).repeat(32)
    a = np.empty((k // 512, 16))
    for p in range(k // 512):
        a[p, :8] = np.random.permutation(np.resize(levels, 8))
        for g in range(8):
            far = levels[np.abs(levels - a[p, g]) >= 10]
            a[p, g + 8] = far[np.random.randint(len(far))]
    return np.exp2(a.ravel()).repeat(32)


BF16 = ml_dtypes.bfloat16


def bf(x):
    return np.asarray(x, np.float32).astype(BF16)


def f64(x):
    return np.asarray(x).astype(np.float64)


B, HID, UD = 1024, 1024, 512


def sigmoid(v):
    return 1.0 / (1.0 + np.exp(-v))


def draw0():
    s, t, u = mx_kscale(HID), mx_kscale(UD), mx_kscale(UD)
    return {
        "encoder_hidden": bf(np.random.standard_normal((B, HID)) * s),
        "spk_vectors": bf(np.random.standard_normal((B, UD)) * t),
        "adr_vectors": bf(np.random.standard_normal((B, UD)) * u),
        "WA_xp": bf(np.random.standard_normal((UD, HID)) / np.sqrt(HID) / s),
        "WA_hp": bf(np.random.standard_normal((UD, UD)) / np.sqrt(UD) / t),
        "VA_hp": bf(np.random.standard_normal((UD, UD)) / np.sqrt(UD) / u),
        "VA_hh": bf(np.random.standard_normal((UD, UD)) / np.sqrt(UD) / u),
    }


def core(encoder_hidden, spk_vectors, adr_vectors, WA_xp, WA_hp, VA_hp, VA_hh):
    x, hs, ha = f64(encoder_hidden), f64(spk_vectors), f64(adr_vectors)
    p_t = sigmoid((mxq(x, 1, "e4m3") @ mxq(f64(WA_xp), 1, "e4m3").T)
                  + (mxq(hs, 1, "e4m3") @ mxq(f64(WA_hp), 1, "e4m3").T)
                  + (mxq(ha, 1, "e4m3") @ mxq(f64(VA_hp), 1, "e4m3").T))
    return mxq(p_t * ha, 1, "e4m3") @ mxq(f64(VA_hh), 1, "e4m3").T


def e4m3fn_bytes(y):
    return np.clip(np.asarray(y, np.float64), -448.0, 448.0).astype(np.float32).astype(ml_dtypes.float8_e4m3fn).view(np.uint8)


def e4m3fn_values(b):
    return np.asarray(b, np.uint8).view(ml_dtypes.float8_e4m3fn).astype(np.float64)


def setup_inputs():
    d = draw0()
    x0 = np.asarray(d['encoder_hidden']).astype(np.float64)
    s = (np.max(np.abs(x0), axis=(0,), keepdims=True) / 448.0).astype(np.float32)
    out = {}
    for k, v in d.items():
        if k == 'encoder_hidden':
            out['encoder_hidden_bytes'] = e4m3fn_bytes(x0 / s.astype(np.float64))
            out['encoder_hidden_scale'] = s
        else:
            out[k] = v
    return out


def reference(encoder_hidden_bytes, encoder_hidden_scale, spk_vectors, adr_vectors, WA_xp, WA_hp, VA_hp, VA_hh):
    return core(e4m3fn_values(encoder_hidden_bytes) * encoder_hidden_scale.astype(np.float64), spk_vectors, adr_vectors, WA_xp, WA_hp, VA_hp, VA_hh)

@@ -1,0 +1,256 @@
+from contextlib import ExitStack
+
+import concourse.mybir as mybir
+from concourse.masks import make_identity
+
+FLOPS = 2 * 1024 * 512 * (1024 + 512 + 512 + 512)
+
+F32 = mybir.dt.float32
+BF16 = mybir.dt.bfloat16
+U32 = mybir.dt.uint32
+U8 = mybir.dt.uint8
+E4M3 = mybir.dt.float8_e4m3fn
+FP8X4 = mybir.dt.float8_e4m3fn_x4
+MULT = mybir.AluOpType.mult
+SIGMOID = mybir.ActivationFunctionType.Sigmoid
+
+P = 128
+HID = 1024
+UD = 512
+G = 256
+R = G // P
+NG = 4
+T = 4
+
+
+def tile_updatespeaker_pa_kernel(tc, x_bytes, x_scale, spk, adr, wa_xp, wa_hp, va_hp, va_hh, out):
+    nc = tc.nc
+    with ExitStack() as ctx:
+        keep = ctx.enter_context(tc.tile_pool(name="keep", bufs=1))
+        psum = ctx.enter_context(tc.psum_pool(name="psum", bufs=4))
+
+        ident = keep.tile([P, P], F32, name="ident")
+        warm = keep.tile([P, 1], F32, name="warm")
+        scale = keep.tile([P, HID], F32, name="scale")
+        make_identity(nc, ident[:])
+
+        raw = {}
+        grouped = {}
+        codes = {}
+        scales = {}
+        xb8 = {}
+        acc = {}
+        p_sb = {}
+        g_sb = {}
+        banks = {}
+
+        def wtile(name, cols):
+            raw[name] = keep.tile([P, T, cols], BF16, name=name + "_raw")
+            return raw[name]
+
+        ctx.enter_context(tc.manual_schedule())
+
+        nc.vector.memset(warm[:], 0.0)
+        nc.scalar.activation(out=warm[:], in_=warm[:], func=SIGMOID)
+
+        for w, n in (("ws", UD), ("wa", UD), ("wx0", 512), ("wx1", 512), ("wh", UD)):
+            raw[w] = keep.tile([P, T, n], BF16, name=w + "_raw")
+        for g in range(NG):
+            xb8[g] = keep.tile([P, R, HID], U8, name="x8_%d" % g)
+            raw["x%d" % g] = keep.tile([P, R, HID], BF16, name="x%d_raw" % g)
+            raw["s%d" % g] = keep.tile([P, R, UD], BF16, name="s%d_raw" % g)
+            raw["a%d" % g] = keep.tile([P, R, UD], BF16, name="a%d_raw" % g)
+
+        def load(name):
+            if name[:2] == "sc":
+                c = {"sc": (0, HID), "sca": (0, 512), "scb": (512, HID)}[name]
+                nc.sync.dma_start(out=scale[:, c[0]:c[1]], in_=x_scale[:, c[0]:c[1]].rearrange("o k -> (o k)").partition_broadcast(P))
+            elif name[0] == "w":
+                src = {"ws": wa_hp, "wa": va_hp, "wx": wa_xp, "wh": va_hh}[name[:2]]
+                k0 = 512 if name == "wx1" else 0
+                key = name
+                b0, b1 = 0, T
+                if name in ("wsa", "wsb"):
+                    key = "ws"
+                    b0, b1 = (0, 2) if name == "wsa" else (2, 4)
+                v = src.rearrange("(t m) k -> m t k", t=T) if name == "wh" else src.rearrange("(m t) k -> m t k", t=T)
+                nc.sync.dma_start(out=raw[key][:, b0:b1, :], in_=v[:, b0:b1, k0 : k0 + 512])
+            else:
+                src = {"x": x_bytes, "s": spk, "a": adr}[name[0]]
+                g = int(name[1])
+                dst = xb8[g] if name[0] == "x" else raw[name]
+                nc.sync.dma_start(out=dst[:], in_=src.rearrange("(g m r) k -> g m r k", g=NG, r=R)[g])
+
+        def widen(g, r):
+            nc.vector.tensor_tensor(out=raw["x%d" % g][:, r, :], in0=xb8[g][:, r, :].bitcast(E4M3), in1=scale[:], op=MULT)
+
+        def turn(name, src, blocks, word0):
+            bank = psum.tile([P, 4, P], F32, tag="turn", name="turn")
+            words = raw[src][:].bitcast(F32)
+            for i, b in enumerate(blocks):
+                for u in range(2):
+                    nc.tensor.transpose(bank[:, 2 * i + u, :], words[:, b, word0 + u : word0 + 256 : 2], ident[:])
+            banks[name] = bank
+
+        def empty(name, dst, half, eng):
+            o = grouped[dst][:, 1024 * half : 1024 * (half + 1)].bitcast(F32).rearrange("p (r m u) -> p r m u", r=2, u=2)
+            i = banks[name][:].rearrange("p (r u) m -> p r m u", u=2)
+            if eng == "S":
+                nc.scalar.copy(out=o, in_=i)
+            else:
+                nc.vector.tensor_copy(out=o, in_=i)
+
+        def quant(name, c0, c1):
+            nc.vector.quantize_mx(
+                out=codes[name][:, c0:c1].bitcast(FP8X4),
+                scales=scales[name][:, c0:c1],
+                in_=grouped[name][:, 4 * c0 : 4 * c1],
+            )
+
+        def alloc(name, cols):
+            grouped[name] = keep.tile([P, 4 * cols], BF16, name=name + "_grp", align_bytes=64)
+            codes[name] = keep.tile([P, cols], U32, name=name + "_cod", align_bytes=64)
+            scales[name] = keep.tile([P, cols], U8, name=name + "_scl", align_bytes=64)
+
+        for n in ("ws", "wa", "wx0", "wx1", "wh"):
+            alloc(n, 512)
+        for g in range(NG):
+            for n in ("s%d", "a%d", "x%dp0", "x%dp1"):
+                alloc(n % g, G)
+            p_sb[g] = keep.tile([P, T, G], F32, name="p%d" % g)
+            alloc("g%d" % g, G)
+
+        def mm(o, w, t, x, c0, c1, start, stop):
+            nc.tensor.matmul_mx(
+                out=o,
+                lhsT=codes[w][:, P * t : P * (t + 1)].bitcast(FP8X4),
+                lhsT_scale=scales[w][:, P * t : P * (t + 1)],
+                rhs=codes[x][:, c0:c1].bitcast(FP8X4),
+                rhs_scale=scales[x][:, c0:c1],
+                start=start,
+                stop=stop,
+            )
+
+        def passes(g):
+            return (("ws", "s%d" % g), ("wa", "a%d" % g), ("wx0", "x%dp0" % g), ("wx1", "x%dp1" % g))
+
+        def gate(g, r):
+            sl = slice(4 * P * r, 4 * P * (r + 1))
+            nc.vector.tensor_tensor(
+                out=grouped["g%d" % g][:, sl].rearrange("p (c i t) -> p c t i", i=4, t=T),
+                in0=p_sb[g][:, :, P * r : P * (r + 1)].rearrange("p t (c i) -> p c t i", i=4),
+                in1=grouped["a%d" % g][:, sl].rearrange("p (c i t) -> p c t i", i=4, t=T),
+                op=MULT,
+            )
+
+        outs = {}
+
+        def mm_out(bank, g, r, c0, c1):
+            nc.tensor.matmul_mx(
+                out=bank[:, 0 : c1 - c0],
+                lhsT=codes["g%d" % g][:, P * r : P * (r + 1)].bitcast(FP8X4),
+                lhsT_scale=scales["g%d" % g][:, P * r : P * (r + 1)],
+                rhs=codes["wh"][:, c0:c1].bitcast(FP8X4),
+                rhs_scale=scales["wh"][:, c0:c1],
+                start=True,
+                stop=True,
+            )
+
+        def put_out(bank, g, r, c0, c1, eng):
+            o = keep.tile([P, c1 - c0], F32, name="o%d%d%d" % (g, r, c0))
+            if eng == "S":
+                nc.scalar.copy(out=o[:], in_=bank[:, 0 : c1 - c0])
+            else:
+                nc.vector.tensor_copy(out=o[:], in_=bank[:, 0 : c1 - c0])
+            nc.sync.dma_start(out=out.rearrange("(g m r) c -> g r m c", g=NG, r=R)[g, r, :, c0:c1], in_=o[:])
+
+        def step(n, eng):
+            k = n[0]
+            if n[:3] == "sig":
+                g, h = int(n[3]), int(n[4])
+                if g < NG - 1:
+                    nc.scalar.activation(out=p_sb[g][:, 2 * h : 2 * h + 2, :], in_=acc[n[3:]][:].rearrange("p (t n) -> p t n", t=2), func=SIGMOID)
+                elif n[5:]:
+                    q = 0 if n[5] == "a" else 2
+                    nc.scalar.activation(out=p_sb[g][:, q : q + 2, P * h : P * (h + 1)], in_=acc[n[3:]][:, 0 : 2 * P].rearrange("p (t n) -> p t n", t=2), func=SIGMOID)
+                else:
+                    nc.scalar.activation(out=p_sb[g][:, :, P * h : P * (h + 1)], in_=acc[n[3:]][:].rearrange("p (t n) -> p t n", t=T), func=SIGMOID)
+            elif n[:4] == "gate":
+                gate(int(n[4]), int(n[5]))
+            elif k == "T":
+                if n[1] == "x":
+                    turn(n[1:], n[1:3], (0, 1), 256 * int(n[3]))
+                elif n[1] == "w":
+                    h = int(n[-1])
+                    turn(n[1:], n[1:-1], (2 * h, 2 * h + 1), 0)
+                else:
+                    turn(n[1:], n[1:], (0, 1), 0)
+            elif k == "E":
+                if n[1] == "x":
+                    empty(n[1:], n[1:3] + "p" + n[3], 0, eng)
+                elif n[1] == "w":
+                    empty(n[1:], n[1:-1], int(n[-1]), eng)
+                else:
+                    empty(n[1:], n[1:], 0, eng)
+            elif k == "Q":
+                if n[1] == "x":
+                    quant(n[1:3] + "p" + n[3], 0, G)
+                elif n[1] == "w":
+                    h = int(n[-1])
+                    quant(n[1:-1], 256 * h, 256 * (h + 1))
+                elif n[1] == "g":
+                    quant(n[1:3], P * int(n[3]), P * (int(n[3]) + 1))
+                else:
+                    quant(n[1:], 0, G)
+            elif k == "W":
+                g, r = int(n[1]), int(n[2])
+                c0, c1 = (512 * int(n[3]), 512 * int(n[3]) + 512) if n[3:] else (0, HID)
+                nc.vector.tensor_tensor(out=raw["x%d" % g][:, r, c0:c1], in0=xb8[g][:, r, c0:c1].bitcast(E4M3), in1=scale[:, c0:c1], op=MULT)
+            elif k == "M":
+                g, h = int(n[1]), int(n[2])
+                bank = psum.tile([P, 512], F32, tag="acc", name="acc")
+                acc[n[1:]] = bank
+                if g < NG - 1:
+                    for i in range(2):
+                        for kk, (w, x) in enumerate(passes(g)):
+                            mm(bank[:, G * i : G * (i + 1)], w, 2 * h + i, x, 0, G, kk == 0, kk == 3)
+                else:
+                    ts = range(T) if not n[3:] else (0, 1) if n[3] == "a" else (2, 3)
+                    for i, t in enumerate(ts):
+                        for kk, (w, x) in enumerate(passes(g)):
+                            mm(bank[:, P * i : P * (i + 1)], w, t, x, P * h, P * (h + 1), kk == 0, kk == 3)
+            elif k == "O":
+                g, r = int(n[1]), int(n[2])
+                if n == "O31":
+                    for i in range(2):
+                        bank = psum.tile([P, 512], F32, tag="acc", name="acc")
+                        outs[3, 1, i] = bank
+                        mm_out(bank, g, r, 256 * i, 256 * (i + 1))
+                else:
+                    bank = psum.tile([P, 512], F32, tag="acc", name="acc")
+                    outs[g, r] = bank
+                    mm_out(bank, g, r, 0, 512)
+            elif k == "P":
+                if n in ("Pa", "Pb"):
+                    i = 0 if n == "Pa" else 1
+                    put_out(outs[3, 1, i], 3, 1, 256 * i, 256 * (i + 1), "SV"[i])
+                else:
+                    put_out(outs[int(n[1]), int(n[2])], int(n[1]), int(n[2]), 0, 512, eng)
+
+        for name in "x0 a0 sca s0 scb wsa wx1 wa wsb x1 wx0 s1 a1 wh a2 s3 x2 x3 s2 a3".split(" "):
+            load(name)
+        program = (
+            "Ta0 W000 Ts0 W010 W001 Tx00 Es0 W011 Tws0 Ex00 Ea0:V Tx01 Ews0 Qx00 "
+            "Twx10 Ex01 Ewx10:V Twa0 Qx01 Tws1 Ewa0 Twa1 W10 Ews1 Twx11 Ewa1 W11 Twx00 "
+            "Ewx11 Twx01 Ewx00 Qa0 Ta1 Ewx01 Qws0 Ts1 Qws1 Qs0 Twh0 Qwa0 Es1 Qwa1 "
+            "Twh1 Qwx00 Ewh0 Qwx01 Tx10 Qwx10 Ewh1 Qwx11 Tx11 Ea1 W20 M00 Ex10 Ex11 "
+            "Qx10 W21 M01 sig00 Qx11 Ta2 sig01 Qwh0 Qwh1 Ts2 Qa1 Qs1 Tx20 Es2 "
+            "gate00 M10 Ea2 Qg00 gate01 Ex20 O00 sig10 Qg01 M11 Qx20 W30 P00 O01 "
+            "sig11 Tx21 W31 P01 Ta3 Ex21 Ts3 Qx21 Tx30 Es3 Qa2 Tx31 Qs2 Ea3 "
+            "gate10 M20 Ex30 Qg10 gate11 Ex31 O10 sig20 M21 Qg11 Qx30 P10 Qx31 Qa3 "
+            "O11 Qs3 sig21 M30 P11 gate20 M31a Qg20 gate21 sig30 O20 sig31a M31b Qg21 "
+            "P20 gate30 O21 sig31b Qg30 P21 gate31 O30 P30 Qg31 O31 Pb Pa "
+        )
+        for n in program.split(" "):
+            if n:
+                step(n.split(":")[0], "V" if ":" in n else "S")

@@ -21,6 +21,9 @@ G = 256
 R = G // P
 NG = 4
 T = 4
+DUM = (3, 1, 1)
+FIRST = "ws"
+LAST = "wx1"
 
 
 def tile_updatespeaker_pa_kernel(tc, x_bytes, x_scale, spk, adr, wa_xp, wa_hp, va_hp, va_hh, out):
@@ -33,6 +36,10 @@ def tile_updatespeaker_pa_kernel(tc, x_bytes, x_scale, spk, adr, wa_xp, wa_hp, v
         warm = keep.tile([P, 1], F32, name="warm")
         scale = keep.tile([P, HID], F32, name="scale")
         make_identity(nc, ident[:])
+        scv = keep.tile([P, 2, 4], F32, name="scv")
+        zero = keep.tile([P, 512], BF16, name="zero")
+        nc.vector.memset(zero[:], 0.0)
+        dummies = []
 
         raw = {}
         grouped = {}
@@ -62,9 +69,8 @@ def tile_updatespeaker_pa_kernel(tc, x_bytes, x_scale, spk, adr, wa_xp, wa_hp, v
             raw["a%d" % g] = keep.tile([P, R, UD], BF16, name="a%d_raw" % g)
 
         def load(name):
-            if name[:2] == "sc":
-                c = {"sc": (0, HID), "sca": (0, 512), "scb": (512, HID)}[name]
-                nc.sync.dma_start(out=scale[:, c[0]:c[1]], in_=x_scale[:, c[0]:c[1]].rearrange("o k -> (o k)").partition_broadcast(P))
+            if name == "sc":
+                nc.sync.dma_start(out=scv[:], in_=x_scale.rearrange("o (h p c) -> p (o h) c", p=P, c=4))
             elif name[0] == "w":
                 src = {"ws": wa_hp, "wa": va_hp, "wx": wa_xp, "wh": va_hh}[name[:2]]
                 k0 = 512 if name == "wx1" else 0
@@ -84,8 +90,29 @@ def tile_updatespeaker_pa_kernel(tc, x_bytes, x_scale, spk, adr, wa_xp, wa_hp, v
         def widen(g, r):
             nc.vector.tensor_tensor(out=raw["x%d" % g][:, r, :], in0=xb8[g][:, r, :].bitcast(E4M3), in1=scale[:], op=MULT)
 
+        def drain_dummies(bank):
+            for i in range(sum(dummies)):
+                nc.tensor.matmul(bank[:].rearrange("p a b -> p (a b)"), lhsT=zero[:, 0:P], rhs=zero[:], start=True, stop=True)
+            dummies.clear()
+
+        def turn_scale(h):
+            bank = psum.tile([P, 4, P], F32, tag="turn", name="turn")
+            drain_dummies(bank)
+            for c in range(4):
+                nc.tensor.transpose(bank[:, c, :], scv[:, h, c : c + 1].to_broadcast([P, P]), ident[:])
+            banks["c%d" % h] = bank
+
+        def empty_scale(h, eng):
+            o = scale[:, 512 * h : 512 * (h + 1)].rearrange("m (p c) -> m p c", c=4)
+            i = banks["c%d" % h][:].rearrange("m c p -> m p c")
+            if eng == "S":
+                nc.scalar.copy(out=o, in_=i)
+            else:
+                nc.vector.tensor_copy(out=o, in_=i)
+
         def turn(name, src, blocks, word0):
             bank = psum.tile([P, 4, P], F32, tag="turn", name="turn")
+            drain_dummies(bank)
             words = raw[src][:].bitcast(F32)
             for i, b in enumerate(blocks):
                 for u in range(2):
@@ -167,8 +194,11 @@ def tile_updatespeaker_pa_kernel(tc, x_bytes, x_scale, spk, adr, wa_xp, wa_hp, v
         def step(n, eng):
             k = n[0]
             if n[:3] == "sig":
-                g, h = int(n[3]), int(n[4])
-                if g < NG - 1:
+                g, h = int(n[3]), int(n[4:5] or "0")
+                if n == "sig0":
+                    for t in range(T):
+                        nc.scalar.activation(out=p_sb[0][:, t, :], in_=acc["0%d" % t][:, 0:G], func=SIGMOID)
+                elif g < NG - 1:
                     nc.scalar.activation(out=p_sb[g][:, 2 * h : 2 * h + 2, :], in_=acc[n[3:]][:].rearrange("p (t n) -> p t n", t=2), func=SIGMOID)
                 elif n[5:]:
                     q = 0 if n[5] == "a" else 2
@@ -177,8 +207,12 @@ def tile_updatespeaker_pa_kernel(tc, x_bytes, x_scale, spk, adr, wa_xp, wa_hp, v
                     nc.scalar.activation(out=p_sb[g][:, :, P * h : P * (h + 1)], in_=acc[n[3:]][:].rearrange("p (t n) -> p t n", t=T), func=SIGMOID)
             elif n[:4] == "gate":
                 gate(int(n[4]), int(n[5]))
+            elif k == "D":
+                dummies.append(DUM[int(n[1])])
             elif k == "T":
-                if n[1] == "x":
+                if n[1] == "c":
+                    turn_scale(int(n[2]))
+                elif n[1] == "x":
                     turn(n[1:], n[1:3], (0, 1), 256 * int(n[3]))
                 elif n[1] == "w":
                     h = int(n[-1])
@@ -186,7 +220,9 @@ def tile_updatespeaker_pa_kernel(tc, x_bytes, x_scale, spk, adr, wa_xp, wa_hp, v
                 else:
                     turn(n[1:], n[1:], (0, 1), 0)
             elif k == "E":
-                if n[1] == "x":
+                if n[1] == "c":
+                    empty_scale(int(n[2]), eng)
+                elif n[1] == "x":
                     empty(n[1:], n[1:3] + "p" + n[3], 0, eng)
                 elif n[1] == "w":
                     empty(n[1:], n[1:-1], int(n[-1]), eng)
@@ -206,6 +242,14 @@ def tile_updatespeaker_pa_kernel(tc, x_bytes, x_scale, spk, adr, wa_xp, wa_hp, v
                 g, r = int(n[1]), int(n[2])
                 c0, c1 = (512 * int(n[3]), 512 * int(n[3]) + 512) if n[3:] else (0, HID)
                 nc.vector.tensor_tensor(out=raw["x%d" % g][:, r, c0:c1], in0=xb8[g][:, r, c0:c1].bitcast(E4M3), in1=scale[:, c0:c1], op=MULT)
+            elif n[:2] == "M0":
+                w = n[2:]
+                first = w == FIRST
+                for t in range(T):
+                    if first:
+                        bank = psum.tile([P, 512], F32, tag="acc", name="acc")
+                        acc["0%d" % t] = bank
+                    mm(acc["0%d" % t][:, 0:G], w, t, {"ws": "s0", "wa": "a0", "wx0": "x0p0", "wx1": "x0p1"}[w], 0, G, first, w == LAST)
             elif k == "M":
                 g, h = int(n[1]), int(n[2])
                 bank = psum.tile([P, 512], F32, tag="acc", name="acc")
@@ -237,19 +281,20 @@ def tile_updatespeaker_pa_kernel(tc, x_bytes, x_scale, spk, adr, wa_xp, wa_hp, v
                 else:
                     put_out(outs[int(n[1]), int(n[2])], int(n[1]), int(n[2]), 0, 512, eng)
 
-        for name in "x0 a0 sca s0 scb wsa wx1 wa wsb x1 wx0 s1 a1 wh a2 s3 x2 x3 s2 a3".split(" "):
+        for name in "sc wsa wsb s0 wa x1 a0 s2 x0 wx0 wx1 x3 a2 wh s1 x2 a1 s3 a3".split(" "):
             load(name)
         program = (
-            "Ta0 W000 Ts0 W010 W001 Tx00 Es0 W011 Tws0 Ex00 Ea0:V Tx01 Ews0 Qx00 "
-            "Twx10 Ex01 Ewx10:V Twa0 Qx01 Tws1 Ewa0 Twa1 W10 Ews1 Twx11 Ewa1 W11 Twx00 "
-            "Ewx11 Twx01 Ewx00 Qa0 Ta1 Ewx01 Qws0 Ts1 Qws1 Qs0 Twh0 Qwa0 Es1 Qwa1 "
-            "Twh1 Qwx00 Ewh0 Qwx01 Tx10 Qwx10 Ewh1 Qwx11 Tx11 Ea1 W20 M00 Ex10 Ex11 "
-            "Qx10 W21 M01 sig00 Qx11 Ta2 sig01 Qwh0 Qwh1 Ts2 Qa1 Qs1 Tx20 Es2 "
-            "gate00 M10 Ea2 Qg00 gate01 Ex20 O00 sig10 Qg01 M11 Qx20 W30 P00 O01 "
-            "sig11 Tx21 W31 P01 Ta3 Ex21 Ts3 Qx21 Tx30 Es3 Qa2 Tx31 Qs2 Ea3 "
-            "gate10 M20 Ex30 Qg10 gate11 Ex31 O10 sig20 M21 Qg11 Qx30 P10 Qx31 Qa3 "
-            "O11 Qs3 sig21 M30 P11 gate20 M31a Qg20 gate21 sig30 O20 sig31a M31b Qg21 "
-            "P20 gate30 O21 sig31b Qg30 P21 gate31 O30 P30 Qg31 O31 Pb Pa "
+            "D0 Tc0 Tws0 Tws1 Ews0:V Ts0 Ews1 Qws0 Tc1 Ec0 Es0:V Twa0 Qs0 Ta0 "
+            "Qws1 Ewa0:V M0ws W000 Ea0 W010 Ec1 Twa1 Qwa0 Qa0 Tx00 Ewa1:V D1 Ex00 "
+            "Twx00 Qwa1 W11 Twx11 Twx01 Ewx11 W011 Twx10 Ewx00 W001 M0wa Ewx10 W10 Tx01 "
+            "Ewx01 Ta1 Ex01 Qx00 Twh1 Qwx11 Ea1 Qwx00 D2 Qwx10 Tx11 Qwx01 W20 Tx10 "
+            "Ex11 Ts1 Ex10 Qx01 M0wx0 Qa1 Es1 Qx11 M0wx1 Ewh1 W21 Twh0 sig0 Qx10 "
+            "Tx21 Qs1 Qwh1 Tx20 Ex21 W30 M11 Ex20 Ewh0 gate01 Ts2 gate00 sig11 Ta2 "
+            "Es2 Qg00 Qg01 M10 Qx21 Ea2 Qx20 Qwh0 Qs2 Qa2 O00 W31 M21 Tx30 "
+            "sig21 Ta3 Ex30 Ts3 Ea3:V sig10 Tx31 Qx30 Es3 gate10 O01 Ex31 M20 gate11 "
+            "P01 Qg11 Qg10 Qs3 sig20 O10 Qx31 O11 Qa3 P10 gate21 M30 P11 Qg21 "
+            "gate20 M31b sig30 Qg20 P00:V M31a sig31b gate30 O21 sig31a O20 P21 Qg30 gate31 "
+            "O30 P20 Qg31 P30 O31 Pa Pb "
         )
         for n in program.split(" "):
             if n:

@@ -21,7 +21,7 @@ G = 256
 R = G // P
 NG = 4
 T = 4
-DUM = (3, 1, 1)
+DUM = (4, 2, 1)
 FIRST = "ws"
 LAST = "wx1"
 
@@ -60,35 +60,38 @@ def tile_updatespeaker_pa_kernel(tc, x_bytes, x_scale, spk, adr, wa_xp, wa_hp, v
         nc.vector.memset(warm[:], 0.0)
         nc.scalar.activation(out=warm[:], in_=warm[:], func=SIGMOID)
 
-        for w, n in (("ws", UD), ("wa", UD), ("wx0", 512), ("wx1", 512), ("wh", UD)):
+        for w, n in (("ws", UD), ("wa", UD), ("wx", HID), ("wh", UD)):
             raw[w] = keep.tile([P, T, n], BF16, name=w + "_raw")
-        for g in range(NG):
-            xb8[g] = keep.tile([P, R, HID], U8, name="x8_%d" % g)
-            raw["x%d" % g] = keep.tile([P, R, HID], BF16, name="x%d_raw" % g)
-            raw["s%d" % g] = keep.tile([P, R, UD], BF16, name="s%d_raw" % g)
-            raw["a%d" % g] = keep.tile([P, R, UD], BF16, name="a%d_raw" % g)
+        for h in range(2):
+            x8 = keep.tile([P, 4, HID], U8, name="x8_%d" % h)
+            xw = keep.tile([P, 4, HID], BF16, name="xw_%d" % h)
+            sp = keep.tile([P, 4, UD], BF16, name="sp_%d" % h)
+            ad = keep.tile([P, 4, UD], BF16, name="ad_%d" % h)
+            for i in range(2):
+                xb8[2 * h + i] = x8[:, 2 * i : 2 * i + 2, :]
+                raw["x%d" % (2 * h + i)] = xw[:, 2 * i : 2 * i + 2, :]
+                raw["s%d" % (2 * h + i)] = sp[:, 2 * i : 2 * i + 2, :]
+                raw["a%d" % (2 * h + i)] = ad[:, 2 * i : 2 * i + 2, :]
+            raw["x%d%d" % (2 * h, 2 * h + 1)] = x8
+            raw["s%d%d" % (2 * h, 2 * h + 1)] = sp
+            raw["a%d%d" % (2 * h, 2 * h + 1)] = ad
 
         def load(name):
             if name == "sc":
                 nc.sync.dma_start(out=scv[:], in_=x_scale.rearrange("o (h p c) -> p (o h) c", p=P, c=4))
             elif name[0] == "w":
                 src = {"ws": wa_hp, "wa": va_hp, "wx": wa_xp, "wh": va_hh}[name[:2]]
-                k0 = 512 if name == "wx1" else 0
-                key = name
-                b0, b1 = 0, T
-                if name in ("wsa", "wsb"):
-                    key = "ws"
-                    b0, b1 = (0, 2) if name == "wsa" else (2, 4)
+                b0, b1 = {"": (0, 4), "A": (0, 2), "B": (2, 4)}[name[2:]]
                 v = src.rearrange("(t m) k -> m t k", t=T) if name == "wh" else src.rearrange("(m t) k -> m t k", t=T)
-                nc.sync.dma_start(out=raw[key][:, b0:b1, :], in_=v[:, b0:b1, k0 : k0 + 512])
+                nc.sync.dma_start(out=raw[name[:2]][:, b0:b1, :], in_=v[:, b0:b1, :])
             else:
-                src = {"x": x_bytes, "s": spk, "a": adr}[name[0]]
+                src = {"x": x_bytes, "s": spk, "a": adr}[name[0]].rearrange("(h m r) k -> h m r k", h=2, r=4)
                 g = int(name[1])
-                dst = xb8[g] if name[0] == "x" else raw[name]
-                nc.sync.dma_start(out=dst[:], in_=src.rearrange("(g m r) k -> g m r k", g=NG, r=R)[g])
-
-        def widen(g, r):
-            nc.vector.tensor_tensor(out=raw["x%d" % g][:, r, :], in0=xb8[g][:, r, :].bitcast(E4M3), in1=scale[:], op=MULT)
+                if name[2:]:
+                    nc.sync.dma_start(out=raw[name][:], in_=src[g // 2])
+                else:
+                    dst = xb8[g] if name[0] == "x" else raw[name]
+                    nc.sync.dma_start(out=dst, in_=src[g // 2, :, 2 * (g % 2) : 2 * (g % 2) + 2, :])
 
         def drain_dummies(bank):
             for i in range(sum(dummies)):
@@ -113,7 +116,7 @@ def tile_updatespeaker_pa_kernel(tc, x_bytes, x_scale, spk, adr, wa_xp, wa_hp, v
         def turn(name, src, blocks, word0):
             bank = psum.tile([P, 4, P], F32, tag="turn", name="turn")
             drain_dummies(bank)
-            words = raw[src][:].bitcast(F32)
+            words = (raw[src][:] if src[0] == "w" else raw[src]).bitcast(F32)
             for i, b in enumerate(blocks):
                 for u in range(2):
                     nc.tensor.transpose(bank[:, 2 * i + u, :], words[:, b, word0 + u : word0 + 256 : 2], ident[:])
@@ -142,12 +145,14 @@ def tile_updatespeaker_pa_kernel(tc, x_bytes, x_scale, spk, adr, wa_xp, wa_hp, v
         for n in ("ws", "wa", "wx0", "wx1", "wh"):
             alloc(n, 512)
         for g in range(NG):
-            for n in ("s%d", "a%d", "x%dp0", "x%dp1"):
-                alloc(n % g, G)
+            alloc("sa%d" % g, 2 * G)
+            alloc("x%d" % g, 2 * G)
             p_sb[g] = keep.tile([P, T, G], F32, name="p%d" % g)
             alloc("g%d" % g, G)
 
-        def mm(o, w, t, x, c0, c1, start, stop):
+        def mm(o, w, t, xc, c0, c1, start, stop):
+            x, base = xc
+            c0, c1 = base + c0, base + c1
             nc.tensor.matmul_mx(
                 out=o,
                 lhsT=codes[w][:, P * t : P * (t + 1)].bitcast(FP8X4),
@@ -159,14 +164,16 @@ def tile_updatespeaker_pa_kernel(tc, x_bytes, x_scale, spk, adr, wa_xp, wa_hp, v
             )
 
         def passes(g):
-            return (("ws", "s%d" % g), ("wa", "a%d" % g), ("wx0", "x%dp0" % g), ("wx1", "x%dp1" % g))
+            return (("ws", ("sa%d" % g, 0)), ("wa", ("sa%d" % g, G)), ("wx0", ("x%d" % g, 0)), ("wx1", ("x%d" % g, G)))
 
-        def gate(g, r):
-            sl = slice(4 * P * r, 4 * P * (r + 1))
+        def gate(g, c0, c1):
+            def quads(ap):
+                return ap.rearrange("p (c i t) -> p c t i", i=4, t=T)
+
             nc.vector.tensor_tensor(
-                out=grouped["g%d" % g][:, sl].rearrange("p (c i t) -> p c t i", i=4, t=T),
-                in0=p_sb[g][:, :, P * r : P * (r + 1)].rearrange("p t (c i) -> p c t i", i=4),
-                in1=grouped["a%d" % g][:, sl].rearrange("p (c i t) -> p c t i", i=4, t=T),
+                out=quads(grouped["g%d" % g][:, 4 * c0 : 4 * c1]),
+                in0=p_sb[g][:, :, c0:c1].rearrange("p t (c i) -> p c t i", i=4),
+                in1=quads(grouped["sa%d" % g][:, 4 * G + 4 * c0 : 4 * G + 4 * c1]),
                 op=MULT,
             )
 
@@ -189,7 +196,7 @@ def tile_updatespeaker_pa_kernel(tc, x_bytes, x_scale, spk, adr, wa_xp, wa_hp, v
                 nc.scalar.copy(out=o[:], in_=bank[:, 0 : c1 - c0])
             else:
                 nc.vector.tensor_copy(out=o[:], in_=bank[:, 0 : c1 - c0])
-            nc.sync.dma_start(out=out.rearrange("(g m r) c -> g r m c", g=NG, r=R)[g, r, :, c0:c1], in_=o[:])
+            nc.sync.dma_start(out=out.rearrange("(h m r) c -> h r m c", h=2, r=4)[g // 2, 2 * (g % 2) + r, :, c0:c1], in_=o[:])
 
         def step(n, eng):
             k = n[0]
@@ -206,7 +213,11 @@ def tile_updatespeaker_pa_kernel(tc, x_bytes, x_scale, spk, adr, wa_xp, wa_hp, v
                 else:
                     nc.scalar.activation(out=p_sb[g][:, :, P * h : P * (h + 1)], in_=acc[n[3:]][:].rearrange("p (t n) -> p t n", t=T), func=SIGMOID)
             elif n[:4] == "gate":
-                gate(int(n[4]), int(n[5]))
+                g = int(n[4])
+                if n[5:]:
+                    gate(g, P * int(n[5]), P * (int(n[5]) + 1))
+                else:
+                    gate(g, 0, G)
             elif k == "D":
                 dummies.append(DUM[int(n[1])])
             elif k == "T":
@@ -216,28 +227,37 @@ def tile_updatespeaker_pa_kernel(tc, x_bytes, x_scale, spk, adr, wa_xp, wa_hp, v
                     turn(n[1:], n[1:3], (0, 1), 256 * int(n[3]))
                 elif n[1] == "w":
                     h = int(n[-1])
-                    turn(n[1:], n[1:-1], (2 * h, 2 * h + 1), 0)
+                    turn(n[1:], n[1:3], (2 * h, 2 * h + 1), 256 if n[1:4] == "wx1" else 0)
                 else:
                     turn(n[1:], n[1:], (0, 1), 0)
             elif k == "E":
                 if n[1] == "c":
                     empty_scale(int(n[2]), eng)
                 elif n[1] == "x":
-                    empty(n[1:], n[1:3] + "p" + n[3], 0, eng)
+                    empty(n[1:], n[1:3], int(n[3]), eng)
                 elif n[1] == "w":
                     empty(n[1:], n[1:-1], int(n[-1]), eng)
                 else:
-                    empty(n[1:], n[1:], 0, eng)
+                    empty(n[1:], "sa" + n[2], "sa".index(n[1]), eng)
             elif k == "Q":
-                if n[1] == "x":
-                    quant(n[1:3] + "p" + n[3], 0, G)
-                elif n[1] == "w":
-                    h = int(n[-1])
-                    quant(n[1:-1], 256 * h, 256 * (h + 1))
-                elif n[1] == "g":
-                    quant(n[1:3], P * int(n[3]), P * (int(n[3]) + 1))
+                m = n[1:]
+                if m[0] == "w":
+                    quant(m, 0, 512)
+                elif m[0] == "g":
+                    if m[2:]:
+                        quant(m[:2], P * int(m[2]), P * (int(m[2]) + 1))
+                    else:
+                        quant(m, 0, G)
+                elif m[:2] == "sa":
+                    quant(m, 0, 2 * G)
+                elif m == "s0":
+                    quant("sa0", 0, G)
+                elif m == "a0":
+                    quant("sa0", G, 2 * G)
+                elif m[2:]:
+                    quant("x0", G * int(m[2]), G * (int(m[2]) + 1))
                 else:
-                    quant(n[1:], 0, G)
+                    quant(m, 0, 2 * G)
             elif k == "W":
                 g, r = int(n[1]), int(n[2])
                 c0, c1 = (512 * int(n[3]), 512 * int(n[3]) + 512) if n[3:] else (0, HID)
@@ -249,7 +269,7 @@ def tile_updatespeaker_pa_kernel(tc, x_bytes, x_scale, spk, adr, wa_xp, wa_hp, v
                     if first:
                         bank = psum.tile([P, 512], F32, tag="acc", name="acc")
                         acc["0%d" % t] = bank
-                    mm(acc["0%d" % t][:, 0:G], w, t, {"ws": "s0", "wa": "a0", "wx0": "x0p0", "wx1": "x0p1"}[w], 0, G, first, w == LAST)
+                    mm(acc["0%d" % t][:, 0:G], w, t, dict(passes(0))[w], 0, G, first, w == LAST)
             elif k == "M":
                 g, h = int(n[1]), int(n[2])
                 bank = psum.tile([P, 512], F32, tag="acc", name="acc")
@@ -281,20 +301,19 @@ def tile_updatespeaker_pa_kernel(tc, x_bytes, x_scale, spk, adr, wa_xp, wa_hp, v
                 else:
                     put_out(outs[int(n[1]), int(n[2])], int(n[1]), int(n[2]), 0, 512, eng)
 
-        for name in "sc wsa wsb s0 wa x1 a0 s2 x0 wx0 wx1 x3 a2 wh s1 x2 a1 s3 a3".split(" "):
+        for name in "wsA s0 sc a0 wsB x0 wa x1 s1 wxA wxB a23 a1 x23 wh s23".split(" "):
             load(name)
         program = (
-            "D0 Tc0 Tws0 Tws1 Ews0:V Ts0 Ews1 Qws0 Tc1 Ec0 Es0:V Twa0 Qs0 Ta0 "
-            "Qws1 Ewa0:V M0ws W000 Ea0 W010 Ec1 Twa1 Qwa0 Qa0 Tx00 Ewa1:V D1 Ex00 "
-            "Twx00 Qwa1 W11 Twx11 Twx01 Ewx11 W011 Twx10 Ewx00 W001 M0wa Ewx10 W10 Tx01 "
-            "Ewx01 Ta1 Ex01 Qx00 Twh1 Qwx11 Ea1 Qwx00 D2 Qwx10 Tx11 Qwx01 W20 Tx10 "
-            "Ex11 Ts1 Ex10 Qx01 M0wx0 Qa1 Es1 Qx11 M0wx1 Ewh1 W21 Twh0 sig0 Qx10 "
-            "Tx21 Qs1 Qwh1 Tx20 Ex21 W30 M11 Ex20 Ewh0 gate01 Ts2 gate00 sig11 Ta2 "
-            "Es2 Qg00 Qg01 M10 Qx21 Ea2 Qx20 Qwh0 Qs2 Qa2 O00 W31 M21 Tx30 "
-            "sig21 Ta3 Ex30 Ts3 Ea3:V sig10 Tx31 Qx30 Es3 gate10 O01 Ex31 M20 gate11 "
-            "P01 Qg11 Qg10 Qs3 sig20 O10 Qx31 O11 Qa3 P10 gate21 M30 P11 Qg21 "
-            "gate20 M31b sig30 Qg20 P00:V M31a sig31b gate30 O21 sig31a O20 P21 Qg30 gate31 "
-            "O30 P20 Qg31 P30 O31 Pa Pb "
+            "D0 Tws0 Ts0 Ews0:V Tc0 Es0 Tc1 Ec0 Tws1 W010 Ta0 Ews1 W000 Twa0 "
+            "Ec1 Qws Qs0 Tx00 W11 Twa1 W001 M0ws W011 Ewa1 Ewa0 Ex00:V Ts1 Ea0 "
+            "Qx00 Twx01 Qwa D1 Qa0 Twx11 W10 Tx01 Ewx11 M0wa Ewx01 W20 Tx10 Ex01 "
+            "Twx00 Es1 Qx01 W21 Twx10 Ewx00 D2 Ewx10 Ta1 Qwx0 Tx11 Ea1 Qwx1 Ta2 "
+            "Ex11 M0wx0 Ea2:V Ex10 M0wx1 Qsa1 Twh1 Qx1 sig0 Twh0 W30 Ts2 Ewh0 M11 "
+            "gate0 Es2 Ewh1 Tx21 Qg0 Qsa2 Tx20 Ex21:V Ts3 Ex20 Qwh M10 sig11 Qx2 "
+            "W31 O01 sig10 M20 P01 gate1 Es3 Tx30 Tx31 Ex30 Qg1 Ta3 Ex31 M21 "
+            "Ea3 Qx3 sig20 Qsa3 O11 sig21 O10 P11:V M30 P10 gate2 M31a sig30 O00 "
+            "Qg2 sig31a M31b gate30 P00 O20 sig31b Qg30 P20 O30 gate31 O21 P30 Qg31 "
+            "P21 O31 Pa Pb "
         )
         for n in program.split(" "):
             if n:

@@ -21,7 +21,7 @@ G = 256
 R = G // P
 NG = 4
 T = 4
-DUM = (4, 2, 1)
+DUM = (4,)
 FIRST = "ws"
 LAST = "wx1"
 
@@ -112,6 +112,41 @@ def tile_updatespeaker_pa_kernel(tc, x_bytes, x_scale, spk, adr, wa_xp, wa_hp, v
                 nc.scalar.copy(out=o, in_=i)
             else:
                 nc.vector.tensor_copy(out=o, in_=i)
+
+        ready = {}
+
+        def reorder(r):
+            if r[:2] == "wx":
+                b0 = 0 if r[2] == "A" else 2
+                src = raw["wx"][:, b0 : b0 + 2, :]
+            elif r in ("s23", "a23", "wa", "ws", "wh"):
+                src = raw[r][:]
+            else:
+                src = raw[r]
+            words = src.bitcast(F32).rearrange("p b k -> p (b k)")
+            n = words.shape[1]
+            o = keep.tile([P, n // 256, 2, P], F32, name=r + "_ord")
+            nc.vector.tensor_copy(out=o[:], in_=words.rearrange("p (c w u) -> p c u w", w=P, u=2))
+            if r[:2] == "wx":
+                for p in range(2):
+                    ready["wx%d%d" % (p, "AB".index(r[2]))] = (o, (p, 2 + p))
+            elif r[0] == "w":
+                for h in range(2):
+                    ready[r + "%d" % h] = (o, (2 * h, 2 * h + 1))
+            elif r[2:]:
+                for h in range(2):
+                    ready[r[0] + "%d" % (2 + h)] = (o, (2 * h, 2 * h + 1))
+            else:
+                ready[r] = (o, (0, 1))
+
+        def turn_ready(name):
+            bank = psum.tile([P, 4, P], F32, tag="turn", name="turn")
+            drain_dummies(bank)
+            o, cs = ready[name]
+            for i, c in enumerate(cs):
+                for u in range(2):
+                    nc.tensor.transpose(bank[:, 2 * i + u, :], o[:, c, u, :], ident[:])
+            banks[name] = bank
 
         def turn(name, src, blocks, word0):
             bank = psum.tile([P, 4, P], F32, tag="turn", name="turn")
@@ -218,11 +253,15 @@ def tile_updatespeaker_pa_kernel(tc, x_bytes, x_scale, spk, adr, wa_xp, wa_hp, v
                     gate(g, P * int(n[5]), P * (int(n[5]) + 1))
                 else:
                     gate(g, 0, G)
+            elif k == "R":
+                reorder(n[1:])
             elif k == "D":
                 dummies.append(DUM[int(n[1])])
             elif k == "T":
                 if n[1] == "c":
                     turn_scale(int(n[2]))
+                elif n[1:] in ready:
+                    turn_ready(n[1:])
                 elif n[1] == "x":
                     turn(n[1:], n[1:3], (0, 1), 256 * int(n[3]))
                 elif n[1] == "w":
@@ -301,19 +340,19 @@ def tile_updatespeaker_pa_kernel(tc, x_bytes, x_scale, spk, adr, wa_xp, wa_hp, v
                 else:
                     put_out(outs[int(n[1]), int(n[2])], int(n[1]), int(n[2]), 0, 512, eng)
 
-        for name in "wsA s0 sc a0 wsB x0 wa x1 s1 wxA wxB a23 a1 x23 wh s23".split(" "):
+        for name in "sc ws s0 x0 wa wxA a0 x1 wxB a1 a23 s1 s23 wh x23".split(" "):
             load(name)
         program = (
-            "D0 Tws0 Ts0 Ews0:V Tc0 Es0 Tc1 Ec0 Tws1 W010 Ta0 Ews1 W000 Twa0 "
-            "Ec1 Qws Qs0 Tx00 W11 Twa1 W001 M0ws W011 Ewa1 Ewa0 Ex00:V Ts1 Ea0 "
-            "Qx00 Twx01 Qwa D1 Qa0 Twx11 W10 Tx01 Ewx11 M0wa Ewx01 W20 Tx10 Ex01 "
-            "Twx00 Es1 Qx01 W21 Twx10 Ewx00 D2 Ewx10 Ta1 Qwx0 Tx11 Ea1 Qwx1 Ta2 "
-            "Ex11 M0wx0 Ea2:V Ex10 M0wx1 Qsa1 Twh1 Qx1 sig0 Twh0 W30 Ts2 Ewh0 M11 "
-            "gate0 Es2 Ewh1 Tx21 Qg0 Qsa2 Tx20 Ex21:V Ts3 Ex20 Qwh M10 sig11 Qx2 "
-            "W31 O01 sig10 M20 P01 gate1 Es3 Tx30 Tx31 Ex30 Qg1 Ta3 Ex31 M21 "
-            "Ea3 Qx3 sig20 Qsa3 O11 sig21 O10 P11:V M30 P10 gate2 M31a sig30 O00 "
-            "Qg2 sig31a M31b gate30 P00 O20 sig31b Qg30 P20 O30 gate31 O21 P30 Qg31 "
-            "P21 O31 Pa Pb "
+            "D0 Tc1 Tc0 Tws1 Ec0 Ts0 Ews1:V Tws0 Es0 W000 Twa0 Ews0 W010 Twa1 "
+            "Ec1 Qws Qs0 Tx00 RwxA Ewa1 W001 Ta0 Ex00 W10 Ewa0 M0ws Ea0 W011 "
+            "Twx00 RwxB Tx01 Qx00 Ewx00 Qwa Twx01 Ex01 Ta1 Qa0 Ewx01 Ra23 Twx11 Twx10 "
+            "Qx01 Ewx11 Ts1 Qwx0 Ewx10 M0wa W11 Es1 M0wx0 Ea1 Qwx1 Tx11 Qsa1 Tx10 "
+            "Ex11 Rs23 M0wx1 Ex10 W20 Ta2 sig0 Twh0 Qx1 Ts2 W21 Ewh0 M11 Es2 "
+            "gate0 Tx20 Tx21 Ex20 Qg0 Ta3 W30 Ea2 M10 Ex21 Qsa2 Ts3 sig10 Qx2 "
+            "Twh1 Ea3 W31 M21 sig11 Ewh1 gate1 Tx31 Es3 Tx30 Ex31 Qsa3 M20 Ex30 "
+            "Qwh sig21 Qx3 O00 sig20 O01 Qg1 M31b P00 gate2 M31a P01 O10 sig31b "
+            "M30 sig31a Qg2 P10 gate31 O20 sig30 O21 P20:V O11 gate30 P11 P21 Qg31 "
+            "Qg30 O31 O30 Pa P30:V Pb "
         )
         for n in program.split(" "):
             if n:

from contextlib import ExitStack

import concourse.mybir as mybir
from concourse.masks import make_identity

FLOPS = 2 * 1024 * 512 * (1024 + 512 + 512 + 512)

F32 = mybir.dt.float32
BF16 = mybir.dt.bfloat16
U32 = mybir.dt.uint32
U8 = mybir.dt.uint8
E4M3 = mybir.dt.float8_e4m3fn
FP8X4 = mybir.dt.float8_e4m3fn_x4
MULT = mybir.AluOpType.mult
SIGMOID = mybir.ActivationFunctionType.Sigmoid

P = 128
HID = 1024
UD = 512
G = 256
R = G // P
NG = 4
T = 4
DUM = (4,)
FIRST = "ws"
LAST = "wx1"


def tile_updatespeaker_pa_kernel(tc, x_bytes, x_scale, spk, adr, wa_xp, wa_hp, va_hp, va_hh, out):
    nc = tc.nc
    with ExitStack() as ctx:
        keep = ctx.enter_context(tc.tile_pool(name="keep", bufs=1))
        psum = ctx.enter_context(tc.psum_pool(name="psum", bufs=4))

        ident = keep.tile([P, P], F32, name="ident")
        warm = keep.tile([P, 1], F32, name="warm")
        scale = keep.tile([P, HID], F32, name="scale")
        make_identity(nc, ident[:])
        scv = keep.tile([P, 2, 4], F32, name="scv")
        zero = keep.tile([P, 512], BF16, name="zero")
        nc.vector.memset(zero[:], 0.0)
        dummies = []

        raw = {}
        grouped = {}
        codes = {}
        scales = {}
        xb8 = {}
        acc = {}
        p_sb = {}
        g_sb = {}
        banks = {}

        def wtile(name, cols):
            raw[name] = keep.tile([P, T, cols], BF16, name=name + "_raw")
            return raw[name]

        ctx.enter_context(tc.manual_schedule())

        nc.vector.memset(warm[:], 0.0)
        nc.scalar.activation(out=warm[:], in_=warm[:], func=SIGMOID)

        for w, n in (("ws", UD), ("wa", UD), ("wx", HID), ("wh", UD)):
            raw[w] = keep.tile([P, T, n], BF16, name=w + "_raw")
        for h in range(2):
            x8 = keep.tile([P, 4, HID], U8, name="x8_%d" % h)
            xw = keep.tile([P, 4, HID], BF16, name="xw_%d" % h)
            sp = keep.tile([P, 4, UD], BF16, name="sp_%d" % h)
            ad = keep.tile([P, 4, UD], BF16, name="ad_%d" % h)
            for i in range(2):
                xb8[2 * h + i] = x8[:, 2 * i : 2 * i + 2, :]
                raw["x%d" % (2 * h + i)] = xw[:, 2 * i : 2 * i + 2, :]
                raw["s%d" % (2 * h + i)] = sp[:, 2 * i : 2 * i + 2, :]
                raw["a%d" % (2 * h + i)] = ad[:, 2 * i : 2 * i + 2, :]
            raw["x%d%d" % (2 * h, 2 * h + 1)] = x8
            raw["s%d%d" % (2 * h, 2 * h + 1)] = sp
            raw["a%d%d" % (2 * h, 2 * h + 1)] = ad

        def load(name):
            if name == "sc":
                nc.sync.dma_start(out=scv[:], in_=x_scale.rearrange("o (h p c) -> p (o h) c", p=P, c=4))
            elif name[0] == "w":
                src = {"ws": wa_hp, "wa": va_hp, "wx": wa_xp, "wh": va_hh}[name[:2]]
                b0, b1 = {"": (0, 4), "A": (0, 2), "B": (2, 4)}[name[2:]]
                v = src.rearrange("(t m) k -> m t k", t=T) if name == "wh" else src.rearrange("(m t) k -> m t k", t=T)
                nc.sync.dma_start(out=raw[name[:2]][:, b0:b1, :], in_=v[:, b0:b1, :])
            else:
                src = {"x": x_bytes, "s": spk, "a": adr}[name[0]].rearrange("(h m r) k -> h m r k", h=2, r=4)
                g = int(name[1])
                if name[2:]:
                    nc.sync.dma_start(out=raw[name][:], in_=src[g // 2])
                else:
                    dst = xb8[g] if name[0] == "x" else raw[name]
                    nc.sync.dma_start(out=dst, in_=src[g // 2, :, 2 * (g % 2) : 2 * (g % 2) + 2, :])

        def drain_dummies(bank):
            for i in range(sum(dummies)):
                nc.tensor.matmul(bank[:].rearrange("p a b -> p (a b)"), lhsT=zero[:, 0:P], rhs=zero[:], start=True, stop=True)
            dummies.clear()

        def turn_scale(h):
            bank = psum.tile([P, 4, P], F32, tag="turn", name="turn")
            drain_dummies(bank)
            for c in range(4):
                nc.tensor.transpose(bank[:, c, :], scv[:, h, c : c + 1].to_broadcast([P, P]), ident[:])
            banks["c%d" % h] = bank

        def empty_scale(h, eng):
            o = scale[:, 512 * h : 512 * (h + 1)].rearrange("m (p c) -> m p c", c=4)
            i = banks["c%d" % h][:].rearrange("m c p -> m p c")
            if eng == "S":
                nc.scalar.copy(out=o, in_=i)
            else:
                nc.vector.tensor_copy(out=o, in_=i)

        ready = {}

        def reorder(r):
            if r[:2] == "wx":
                b0 = 0 if r[2] == "A" else 2
                src = raw["wx"][:, b0 : b0 + 2, :]
            elif r in ("s23", "a23", "wa", "ws", "wh"):
                src = raw[r][:]
            else:
                src = raw[r]
            words = src.bitcast(F32).rearrange("p b k -> p (b k)")
            n = words.shape[1]
            o = keep.tile([P, n // 256, 2, P], F32, name=r + "_ord")
            nc.vector.tensor_copy(out=o[:], in_=words.rearrange("p (c w u) -> p c u w", w=P, u=2))
            if r[:2] == "wx":
                for p in range(2):
                    ready["wx%d%d" % (p, "AB".index(r[2]))] = (o, (p, 2 + p))
            elif r[0] == "w":
                for h in range(2):
                    ready[r + "%d" % h] = (o, (2 * h, 2 * h + 1))
            elif r[2:]:
                for h in range(2):
                    ready[r[0] + "%d" % (2 + h)] = (o, (2 * h, 2 * h + 1))
            else:
                ready[r] = (o, (0, 1))

        def turn_ready(name):
            bank = psum.tile([P, 4, P], F32, tag="turn", name="turn")
            drain_dummies(bank)
            o, cs = ready[name]
            for i, c in enumerate(cs):
                for u in range(2):
                    nc.tensor.transpose(bank[:, 2 * i + u, :], o[:, c, u, :], ident[:])
            banks[name] = bank

        def turn(name, src, blocks, word0):
            bank = psum.tile([P, 4, P], F32, tag="turn", name="turn")
            drain_dummies(bank)
            words = (raw[src][:] if src[0] == "w" else raw[src]).bitcast(F32)
            for i, b in enumerate(blocks):
                for u in range(2):
                    nc.tensor.transpose(bank[:, 2 * i + u, :], words[:, b, word0 + u : word0 + 256 : 2], ident[:])
            banks[name] = bank

        def empty(name, dst, half, eng):
            o = grouped[dst][:, 1024 * half : 1024 * (half + 1)].bitcast(F32).rearrange("p (r m u) -> p r m u", r=2, u=2)
            i = banks[name][:].rearrange("p (r u) m -> p r m u", u=2)
            if eng == "S":
                nc.scalar.copy(out=o, in_=i)
            else:
                nc.vector.tensor_copy(out=o, in_=i)

        def quant(name, c0, c1):
            nc.vector.quantize_mx(
                out=codes[name][:, c0:c1].bitcast(FP8X4),
                scales=scales[name][:, c0:c1],
                in_=grouped[name][:, 4 * c0 : 4 * c1],
            )

        def alloc(name, cols):
            grouped[name] = keep.tile([P, 4 * cols], BF16, name=name + "_grp", align_bytes=64)
            codes[name] = keep.tile([P, cols], U32, name=name + "_cod", align_bytes=64)
            scales[name] = keep.tile([P, cols], U8, name=name + "_scl", align_bytes=64)

        for n in ("ws", "wa", "wx0", "wx1", "wh"):
            alloc(n, 512)
        for g in range(NG):
            alloc("sa%d" % g, 2 * G)
            alloc("x%d" % g, 2 * G)
            p_sb[g] = keep.tile([P, T, G], F32, name="p%d" % g)
            alloc("g%d" % g, G)

        def mm(o, w, t, xc, c0, c1, start, stop):
            x, base = xc
            c0, c1 = base + c0, base + c1
            nc.tensor.matmul_mx(
                out=o,
                lhsT=codes[w][:, P * t : P * (t + 1)].bitcast(FP8X4),
                lhsT_scale=scales[w][:, P * t : P * (t + 1)],
                rhs=codes[x][:, c0:c1].bitcast(FP8X4),
                rhs_scale=scales[x][:, c0:c1],
                start=start,
                stop=stop,
            )

        def passes(g):
            return (("ws", ("sa%d" % g, 0)), ("wa", ("sa%d" % g, G)), ("wx0", ("x%d" % g, 0)), ("wx1", ("x%d" % g, G)))

        def gate(g, c0, c1):
            def quads(ap):
                return ap.rearrange("p (c i t) -> p c t i", i=4, t=T)

            nc.vector.tensor_tensor(
                out=quads(grouped["g%d" % g][:, 4 * c0 : 4 * c1]),
                in0=p_sb[g][:, :, c0:c1].rearrange("p t (c i) -> p c t i", i=4),
                in1=quads(grouped["sa%d" % g][:, 4 * G + 4 * c0 : 4 * G + 4 * c1]),
                op=MULT,
            )

        outs = {}

        def mm_out(bank, g, r, c0, c1):
            nc.tensor.matmul_mx(
                out=bank[:, 0 : c1 - c0],
                lhsT=codes["g%d" % g][:, P * r : P * (r + 1)].bitcast(FP8X4),
                lhsT_scale=scales["g%d" % g][:, P * r : P * (r + 1)],
                rhs=codes["wh"][:, c0:c1].bitcast(FP8X4),
                rhs_scale=scales["wh"][:, c0:c1],
                start=True,
                stop=True,
            )

        def put_out(bank, g, r, c0, c1, eng):
            o = keep.tile([P, c1 - c0], F32, name="o%d%d%d" % (g, r, c0))
            if eng == "S":
                nc.scalar.copy(out=o[:], in_=bank[:, 0 : c1 - c0])
            else:
                nc.vector.tensor_copy(out=o[:], in_=bank[:, 0 : c1 - c0])
            nc.sync.dma_start(out=out.rearrange("(h m r) c -> h r m c", h=2, r=4)[g // 2, 2 * (g % 2) + r, :, c0:c1], in_=o[:])

        def step(n, eng):
            k = n[0]
            if n[:3] == "sig":
                g, h = int(n[3]), int(n[4:5] or "0")
                if n == "sig0":
                    for t in range(T):
                        nc.scalar.activation(out=p_sb[0][:, t, :], in_=acc["0%d" % t][:, 0:G], func=SIGMOID)
                elif g < NG - 1:
                    nc.scalar.activation(out=p_sb[g][:, 2 * h : 2 * h + 2, :], in_=acc[n[3:]][:].rearrange("p (t n) -> p t n", t=2), func=SIGMOID)
                elif n[5:]:
                    q = 0 if n[5] == "a" else 2
                    nc.scalar.activation(out=p_sb[g][:, q : q + 2, P * h : P * (h + 1)], in_=acc[n[3:]][:, 0 : 2 * P].rearrange("p (t n) -> p t n", t=2), func=SIGMOID)
                else:
                    nc.scalar.activation(out=p_sb[g][:, :, P * h : P * (h + 1)], in_=acc[n[3:]][:].rearrange("p (t n) -> p t n", t=T), func=SIGMOID)
            elif n[:4] == "gate":
                g = int(n[4])
                if n[5:]:
                    gate(g, P * int(n[5]), P * (int(n[5]) + 1))
                else:
                    gate(g, 0, G)
            elif k == "R":
                reorder(n[1:])
            elif k == "D":
                dummies.append(DUM[int(n[1])])
            elif k == "T":
                if n[1] == "c":
                    turn_scale(int(n[2]))
                elif n[1:] in ready:
                    turn_ready(n[1:])
                elif n[1] == "x":
                    turn(n[1:], n[1:3], (0, 1), 256 * int(n[3]))
                elif n[1] == "w":
                    h = int(n[-1])
                    turn(n[1:], n[1:3], (2 * h, 2 * h + 1), 256 if n[1:4] == "wx1" else 0)
                else:
                    turn(n[1:], n[1:], (0, 1), 0)
            elif k == "E":
                if n[1] == "c":
                    empty_scale(int(n[2]), eng)
                elif n[1] == "x":
                    empty(n[1:], n[1:3], int(n[3]), eng)
                elif n[1] == "w":
                    empty(n[1:], n[1:-1], int(n[-1]), eng)
                else:
                    empty(n[1:], "sa" + n[2], "sa".index(n[1]), eng)
            elif k == "Q":
                m = n[1:]
                if m[0] == "w":
                    quant(m, 0, 512)
                elif m[0] == "g":
                    if m[2:]:
                        quant(m[:2], P * int(m[2]), P * (int(m[2]) + 1))
                    else:
                        quant(m, 0, G)
                elif m[:2] == "sa":
                    quant(m, 0, 2 * G)
                elif m == "s0":
                    quant("sa0", 0, G)
                elif m == "a0":
                    quant("sa0", G, 2 * G)
                elif m[2:]:
                    quant("x0", G * int(m[2]), G * (int(m[2]) + 1))
                else:
                    quant(m, 0, 2 * G)
            elif k == "W":
                g, r = int(n[1]), int(n[2])
                c0, c1 = (512 * int(n[3]), 512 * int(n[3]) + 512) if n[3:] else (0, HID)
                nc.vector.tensor_tensor(out=raw["x%d" % g][:, r, c0:c1], in0=xb8[g][:, r, c0:c1].bitcast(E4M3), in1=scale[:, c0:c1], op=MULT)
            elif n[:2] == "M0":
                w = n[2:]
                first = w == FIRST
                for t in range(T):
                    if first:
                        bank = psum.tile([P, 512], F32, tag="acc", name="acc")
                        acc["0%d" % t] = bank
                    mm(acc["0%d" % t][:, 0:G], w, t, dict(passes(0))[w], 0, G, first, w == LAST)
            elif k == "M":
                g, h = int(n[1]), int(n[2])
                bank = psum.tile([P, 512], F32, tag="acc", name="acc")
                acc[n[1:]] = bank
                if g < NG - 1:
                    for i in range(2):
                        for kk, (w, x) in enumerate(passes(g)):
                            mm(bank[:, G * i : G * (i + 1)], w, 2 * h + i, x, 0, G, kk == 0, kk == 3)
                else:
                    ts = range(T) if not n[3:] else (0, 1) if n[3] == "a" else (2, 3)
                    for i, t in enumerate(ts):
                        for kk, (w, x) in enumerate(passes(g)):
                            mm(bank[:, P * i : P * (i + 1)], w, t, x, P * h, P * (h + 1), kk == 0, kk == 3)
            elif k == "O":
                g, r = int(n[1]), int(n[2])
                if n == "O31":
                    for i in range(2):
                        bank = psum.tile([P, 512], F32, tag="acc", name="acc")
                        outs[3, 1, i] = bank
                        mm_out(bank, g, r, 256 * i, 256 * (i + 1))
                else:
                    bank = psum.tile([P, 512], F32, tag="acc", name="acc")
                    outs[g, r] = bank
                    mm_out(bank, g, r, 0, 512)
            elif k == "P":
                if n in ("Pa", "Pb"):
                    i = 0 if n == "Pa" else 1
                    put_out(outs[3, 1, i], 3, 1, 256 * i, 256 * (i + 1), "SV"[i])
                else:
                    put_out(outs[int(n[1]), int(n[2])], int(n[1]), int(n[2]), 0, 512, eng)

        for name in "sc ws s0 x0 wa wxA a0 x1 wxB a1 a23 s1 s23 wh x23".split(" "):
            load(name)
        program = (
            "D0 Tc1 Tc0 Tws1 Ec0 Ts0 Ews1:V Tws0 Es0 W000 Twa0 Ews0 W010 Twa1 "
            "Ec1 Qws Qs0 Tx00 RwxA Ewa1 W001 Ta0 Ex00 W10 Ewa0 M0ws Ea0 W011 "
            "Twx00 RwxB Tx01 Qx00 Ewx00 Qwa Twx01 Ex01 Ta1 Qa0 Ewx01 Ra23 Twx11 Twx10 "
            "Qx01 Ewx11 Ts1 Qwx0 Ewx10 M0wa W11 Es1 M0wx0 Ea1 Qwx1 Tx11 Qsa1 Tx10 "
            "Ex11 Rs23 M0wx1 Ex10 W20 Ta2 sig0 Twh0 Qx1 Ts2 W21 Ewh0 M11 Es2 "
            "gate0 Tx20 Tx21 Ex20 Qg0 Ta3 W30 Ea2 M10 Ex21 Qsa2 Ts3 sig10 Qx2 "
            "Twh1 Ea3 W31 M21 sig11 Ewh1 gate1 Tx31 Es3 Tx30 Ex31 Qsa3 M20 Ex30 "
            "Qwh sig21 Qx3 O00 sig20 O01 Qg1 M31b P00 gate2 M31a P01 O10 sig31b "
            "M30 sig31a Qg2 P10 gate31 O20 sig30 O21 P20:V O11 gate30 P11 P21 Qg31 "
            "Qg30 O31 O30 Pa P30:V Pb "
        )
        for n in program.split(" "):
            if n:
                step(n.split(":")[0], "V" if ":" in n else "S")
